import numpy as np
import ml_dtypes


def mxq(x, axis, fmt="e4m3"):
    dtype, down = {"e4m3": (ml_dtypes.float8_e4m3fn, 7), "e5m2": (ml_dtypes.float8_e5m2, 14)}[fmt]
    v = np.moveaxis(np.asarray(x, np.float32).astype(ml_dtypes.bfloat16).astype(np.float64), axis, -1)
    blocks = v.reshape(v.shape[:-1] + (-1, 32))
    amax = np.abs(blocks).max(-1, keepdims=True)
    byte = np.maximum(np.where(amax > 0, np.frexp(amax)[1] - 1 + 127, 0) - down, 1)
    scale = np.exp2(byte - 127.0)
    codes = (blocks / scale).astype(np.float32).astype(dtype).astype(np.float64)
    return np.moveaxis((codes * scale).reshape(v.shape), -1, axis)


BF16 = ml_dtypes.bfloat16


def bf(x):
    return np.asarray(x, np.float32).astype(BF16)


def f64(x):
    return np.asarray(x).astype(np.float64)


B, K, N = 8192, 512, 512


def binarize(v):
    return np.where(v >= 0, 1.0, -1.0)


def setup_inputs():
    x = np.random.standard_normal((B, K)) * 3.0 / np.sqrt(K)
    w = np.random.standard_normal((K, N)) * 0.6
    g = np.random.standard_normal((B, N)) * np.exp2(np.random.randint(-12, 1, (B, 1))) * 0.5
    return {"x": bf(x), "w": bf(w), "grad_out": bf(g)}


def reference(x, w, grad_out):
    w_c = np.clip(f64(w), -1.0, 1.0)
    w_b = binarize(w_c)
    return mxq(f64(grad_out), 1, "e5m2") @ mxq(w_b, 1, "e4m3").T

@@ -1,0 +1,180 @@
+from contextlib import ExitStack
+
+import concourse.mybir as mybir
+from concourse.masks import make_identity
+
+BF16 = mybir.dt.bfloat16
+F32 = mybir.dt.float32
+U32 = mybir.dt.uint32
+U8 = mybir.dt.uint8
+E5M2X4 = mybir.dt.float8_e5m2_x4
+E4M3X4 = mybir.dt.float8_e4m3fn_x4
+ALU = mybir.AluOpType
+
+P = 128
+TOKENS = 8192
+N_OUT = 512
+K_IN = 512
+SLOTS = TOKENS // P
+G = 4
+NG = SLOTS // G
+STORE_SLOTS = 8
+LOAD_SLOTS = (4, 4, 8, 16, 16, 16)
+SCALAR_OUT = (1, 3, 5)
+O_BUFS = 6
+
+FLOPS = 2 * TOKENS * N_OUT * K_IN
+BYTES = TOKENS * N_OUT * 2 + K_IN * N_OUT * 2 + TOKENS * K_IN * 4
+
+
+def tile_binlinear_t_kernel(tc, x, w, grad_out, out):
+    nc = tc.nc
+    g_view = grad_out.rearrange("(p s) n -> p (s n)", s=SLOTS)
+    o_view = out.rearrange("(p s) k -> p (s k)", s=SLOTS)
+    with ExitStack() as ctx:
+        const = ctx.enter_context(tc.tile_pool(name="const", bufs=1))
+        stage = ctx.enter_context(tc.tile_pool(name="stage", bufs=4))
+        outs = ctx.enter_context(tc.tile_pool(name="outs", bufs=O_BUFS))
+        psum = ctx.enter_context(tc.psum_pool(name="psum", bufs=4))
+        ctx.enter_context(tc.manual_schedule())
+
+        w_sb = const.tile([P, 4 * N_OUT], BF16, name="w_sb")
+        nc.sync.dma_start(
+            out=w_sb[:].rearrange("p (t n) -> p t n", t=4),
+            in_=w.rearrange("(t p) n -> p t n", p=P),
+        )
+        slot_home = []
+        first = 0
+        for i, count in enumerate(LOAD_SLOTS):
+            g_sb = const.tile([P, count * N_OUT], BF16, name="g_sb%d" % i)
+            nc.sync.dma_start(out=g_sb[:], in_=g_view[:, first * N_OUT : (first + count) * N_OUT])
+            words = g_sb[:].bitcast(F32)
+            for j in range(count):
+                slot_home.append((words, j * (N_OUT // 2)))
+            first += count
+
+        ident = const.tile([P, P], F32, name="ident")
+        make_identity(nc, ident[:])
+
+        w_words = w_sb[:].bitcast(F32)
+        w_clip = const.tile([P, 4 * K_IN], F32, name="w_clip")
+        for u in range(2):
+            wt = psum.tile([P, 512], F32, tag="acc")
+            for t in range(4):
+                nc.tensor.transpose(
+                    out=wt[:, t * P : (t + 1) * P],
+                    in_=w_words[:, t * 256 + u * P : t * 256 + (u + 1) * P],
+                    identity=ident[:],
+                )
+            nc.vector.tensor_scalar(
+                out=w_clip[:, u * 1024 : (u + 1) * 1024],
+                in0=wt[:].bitcast(BF16),
+                scalar1=-1.0,
+                scalar2=1.0,
+                op0=ALU.max,
+                op1=ALU.min,
+            )
+        w_two = const.tile([P, 4 * K_IN], F32, name="w_two")
+        nc.vector.tensor_scalar(
+            out=w_two[:], in0=w_clip[:], scalar1=0.0, scalar2=2.0, op0=ALU.is_ge, op1=ALU.mult
+        )
+        w_bin = const.tile([P, 4 * K_IN], BF16, name="w_bin", align_bytes=64)
+        nc.vector.tensor_scalar(
+            out=w_bin[:].rearrange("p (k u e) -> p k u e", u=2, e=2),
+            in0=w_two[:].rearrange("p (u k e) -> p k u e", u=2, e=2),
+            scalar1=-1.0,
+            scalar2=None,
+            op0=ALU.add,
+        )
+        w_codes = const.tile([P, K_IN], U32, name="w_codes", align_bytes=64)
+        w_scales = const.tile([P, K_IN], U8, name="w_scales", align_bytes=64)
+        nc.vector.quantize_mx(out=w_codes[:].bitcast(E4M3X4), scales=w_scales[:], in_=w_bin[:])
+
+        banks_of = {}
+        grouped_of = {}
+        mx_of = {}
+        acc_of = {}
+        o_of = {}
+
+        def transposes(g):
+            banks = []
+            for b in range(G // 2):
+                xt = psum.tile([P, 512], F32, tag="xt")
+                for a in range(2):
+                    words, col = slot_home[g * G + 2 * b + a]
+                    for u in range(2):
+                        nc.tensor.transpose(
+                            out=xt[:, (2 * a + u) * P : (2 * a + u + 1) * P],
+                            in_=words[:, col + u * P : col + (u + 1) * P],
+                            identity=ident[:],
+                        )
+                banks.append(xt)
+            banks_of[g] = banks
+
+        def regroup(g):
+            grouped = stage.tile([P, G * 512], BF16, tag="grouped", align_bytes=64)
+            gw = grouped[:].bitcast(F32)
+            for b, xt in enumerate(banks_of[g]):
+                nc.scalar.copy(
+                    out=gw[:, b * 512 : (b + 1) * 512].rearrange("p (a r u) -> p a r u", a=2, u=2),
+                    in_=xt[:].rearrange("p (a u r) -> p a r u", a=2, u=2),
+                )
+            grouped_of[g] = grouped
+
+        def quantise(g):
+            codes = stage.tile([P, G * P], U32, tag="codes", align_bytes=64)
+            scales = stage.tile([P, G * P], U8, tag="scales", align_bytes=64)
+            nc.vector.quantize_mx(
+                out=codes[:].bitcast(E5M2X4), scales=scales[:], in_=grouped_of[g][:]
+            )
+            mx_of[g] = (codes, scales)
+
+        def multiply(g):
+            codes, scales = mx_of[g]
+            accs = []
+            for a in range(G):
+                acc = psum.tile([P, K_IN], F32, tag="acc")
+                nc.tensor.matmul_mx(
+                    out=acc[:],
+                    lhsT=codes[:, a * P : (a + 1) * P].bitcast(E5M2X4),
+                    lhsT_scale=scales[:, a * P : (a + 1) * P],
+                    rhs=w_codes[:].bitcast(E4M3X4),
+                    rhs_scale=w_scales[:],
+                    start=True,
+                    stop=True,
+                )
+                accs.append(acc)
+            acc_of[g] = accs
+
+        def copy_out(g):
+            for a, acc in enumerate(acc_of[g]):
+                slot = g * G + a
+                chunk, j = divmod(slot, STORE_SLOTS)
+                if j == 0:
+                    o_sb = outs.tile([P, STORE_SLOTS * K_IN], F32, tag="o_sb")
+                    o_of[chunk] = o_sb
+                dst = o_of[chunk][:, j * K_IN : (j + 1) * K_IN]
+                if j in SCALAR_OUT:
+                    nc.scalar.copy(out=dst, in_=acc[:])
+                else:
+                    nc.vector.tensor_copy(out=dst, in_=acc[:])
+                if j == STORE_SLOTS - 1:
+                    nc.sync.dma_start(
+                        out=o_view[:, chunk * STORE_SLOTS * K_IN : (chunk + 1) * STORE_SLOTS * K_IN],
+                        in_=o_of[chunk][:],
+                    )
+
+        for g in range(3):
+            transposes(g)
+            regroup(g)
+        quantise(0)
+        quantise(1)
+        for g in range(NG):
+            multiply(g)
+            if g + 3 < NG:
+                transposes(g + 3)
+            if g + 2 < NG:
+                quantise(g + 2)
+            copy_out(g)
+            if g + 3 < NG:
+                regroup(g + 3)

@@ -18,7 +18,7 @@ K_IN = 512
 SLOTS = TOKENS // P
 G = 4
 NG = SLOTS // G
-STORE_SLOTS = 8
+STORE_PLAN = (8, 8, 8, 8, 8, 8, 8, 4, 4)
 LOAD_SLOTS = (4, 4, 8, 16, 16, 16)
 SCALAR_OUT = (1, 3, 5)
 O_BUFS = 6
@@ -39,10 +39,6 @@ def tile_binlinear_t_kernel(tc, x, w, grad_out, out):
         ctx.enter_context(tc.manual_schedule())
 
         w_sb = const.tile([P, 4 * N_OUT], BF16, name="w_sb")
-        nc.sync.dma_start(
-            out=w_sb[:].rearrange("p (t n) -> p t n", t=4),
-            in_=w.rearrange("(t p) n -> p t n", p=P),
-        )
         slot_home = []
         first = 0
         for i, count in enumerate(LOAD_SLOTS):
@@ -52,43 +48,14 @@ def tile_binlinear_t_kernel(tc, x, w, grad_out, out):
             for j in range(count):
                 slot_home.append((words, j * (N_OUT // 2)))
             first += count
+            if i == 0:
+                nc.sync.dma_start(
+                    out=w_sb[:].rearrange("p (t n) -> p t n", t=4),
+                    in_=w.rearrange("(t p) n -> p t n", p=P),
+                )
 
         ident = const.tile([P, P], F32, name="ident")
         make_identity(nc, ident[:])
-
-        w_words = w_sb[:].bitcast(F32)
-        w_clip = const.tile([P, 4 * K_IN], F32, name="w_clip")
-        for u in range(2):
-            wt = psum.tile([P, 512], F32, tag="acc")
-            for t in range(4):
-                nc.tensor.transpose(
-                    out=wt[:, t * P : (t + 1) * P],
-                    in_=w_words[:, t * 256 + u * P : t * 256 + (u + 1) * P],
-                    identity=ident[:],
-                )
-            nc.vector.tensor_scalar(
-                out=w_clip[:, u * 1024 : (u + 1) * 1024],
-                in0=wt[:].bitcast(BF16),
-                scalar1=-1.0,
-                scalar2=1.0,
-                op0=ALU.max,
-                op1=ALU.min,
-            )
-        w_two = const.tile([P, 4 * K_IN], F32, name="w_two")
-        nc.vector.tensor_scalar(
-            out=w_two[:], in0=w_clip[:], scalar1=0.0, scalar2=2.0, op0=ALU.is_ge, op1=ALU.mult
-        )
-        w_bin = const.tile([P, 4 * K_IN], BF16, name="w_bin", align_bytes=64)
-        nc.vector.tensor_scalar(
-            out=w_bin[:].rearrange("p (k u e) -> p k u e", u=2, e=2),
-            in0=w_two[:].rearrange("p (u k e) -> p k u e", u=2, e=2),
-            scalar1=-1.0,
-            scalar2=None,
-            op0=ALU.add,
-        )
-        w_codes = const.tile([P, K_IN], U32, name="w_codes", align_bytes=64)
-        w_scales = const.tile([P, K_IN], U8, name="w_scales", align_bytes=64)
-        nc.vector.quantize_mx(out=w_codes[:].bitcast(E4M3X4), scales=w_scales[:], in_=w_bin[:])
 
         banks_of = {}
         grouped_of = {}
@@ -96,12 +63,12 @@ def tile_binlinear_t_kernel(tc, x, w, grad_out, out):
         acc_of = {}
         o_of = {}
 
-        def transposes(g):
+        def transposes(g, homes):
             banks = []
             for b in range(G // 2):
                 xt = psum.tile([P, 512], F32, tag="xt")
                 for a in range(2):
-                    words, col = slot_home[g * G + 2 * b + a]
+                    words, col = homes[2 * b + a]
                     for u in range(2):
                         nc.tensor.transpose(
                             out=xt[:, (2 * a + u) * P : (2 * a + u + 1) * P],
@@ -111,14 +78,16 @@ def tile_binlinear_t_kernel(tc, x, w, grad_out, out):
                 banks.append(xt)
             banks_of[g] = banks
 
-        def regroup(g):
+        def regroup(g, share):
             grouped = stage.tile([P, G * 512], BF16, tag="grouped", align_bytes=64)
             gw = grouped[:].bitcast(F32)
             for b, xt in enumerate(banks_of[g]):
-                nc.scalar.copy(
-                    out=gw[:, b * 512 : (b + 1) * 512].rearrange("p (a r u) -> p a r u", a=2, u=2),
-                    in_=xt[:].rearrange("p (a u r) -> p a r u", a=2, u=2),
-                )
+                dst = gw[:, b * 512 : (b + 1) * 512].rearrange("p (a r u) -> p a r u", a=2, u=2)
+                src = xt[:].rearrange("p (a u r) -> p a r u", a=2, u=2)
+                if share and b == 0:
+                    nc.vector.tensor_copy(out=dst, in_=src)
+                else:
+                    nc.scalar.copy(out=dst, in_=src)
             grouped_of[g] = grouped
 
         def quantise(g):
@@ -146,35 +115,67 @@ def tile_binlinear_t_kernel(tc, x, w, grad_out, out):
                 accs.append(acc)
             acc_of[g] = accs
 
+        store_of = []
+        for chunk, count in enumerate(STORE_PLAN):
+            for j in range(count):
+                store_of.append((chunk, j, count))
+
         def copy_out(g):
             for a, acc in enumerate(acc_of[g]):
                 slot = g * G + a
-                chunk, j = divmod(slot, STORE_SLOTS)
+                chunk, j, count = store_of[slot]
                 if j == 0:
-                    o_sb = outs.tile([P, STORE_SLOTS * K_IN], F32, tag="o_sb")
+                    o_sb = outs.tile([P, count * K_IN], F32, tag="o_sb")
                     o_of[chunk] = o_sb
                 dst = o_of[chunk][:, j * K_IN : (j + 1) * K_IN]
-                if j in SCALAR_OUT:
+                if slot % 8 in SCALAR_OUT:
                     nc.scalar.copy(out=dst, in_=acc[:])
                 else:
                     nc.vector.tensor_copy(out=dst, in_=acc[:])
-                if j == STORE_SLOTS - 1:
+                if j == count - 1:
                     nc.sync.dma_start(
-                        out=o_view[:, chunk * STORE_SLOTS * K_IN : (chunk + 1) * STORE_SLOTS * K_IN],
+                        out=o_view[:, (slot + 1 - count) * K_IN : (slot + 1) * K_IN],
                         in_=o_of[chunk][:],
                     )
 
-        for g in range(3):
-            transposes(g)
-            regroup(g)
+        def homes_of(g):
+            return slot_home[g * G : (g + 1) * G]
+
+        transposes(0, homes_of(0))
+        regroup(0, False)
+
+        w_clip = const.tile([P, 4 * N_OUT], BF16, name="w_clip")
+        nc.vector.tensor_scalar(
+            out=w_clip[:], in0=w_sb[:], scalar1=-1.0, scalar2=1.0, op0=ALU.max, op1=ALU.min
+        )
+        w_two = const.tile([P, 4 * N_OUT], BF16, name="w_two")
+        nc.vector.tensor_scalar(
+            out=w_two[:], in0=w_clip[:], scalar1=0.0, scalar2=2.0, op0=ALU.is_ge, op1=ALU.mult
+        )
+        w_bin = const.tile([P, 4 * N_OUT], BF16, name="w_bin")
+        nc.vector.tensor_scalar(
+            out=w_bin[:], in0=w_two[:], scalar1=-1.0, scalar2=None, op0=ALU.add
+        )
+        w_words = w_bin[:].bitcast(F32)
+        transposes("w", [(w_words, t * (N_OUT // 2)) for t in range(4)])
         quantise(0)
+        regroup("w", True)
+        w_codes = const.tile([P, K_IN], U32, name="w_codes", align_bytes=64)
+        w_scales = const.tile([P, K_IN], U8, name="w_scales", align_bytes=64)
+        nc.vector.quantize_mx(
+            out=w_codes[:].bitcast(E4M3X4), scales=w_scales[:], in_=grouped_of["w"][:]
+        )
+
+        for g in (1, 2):
+            transposes(g, homes_of(g))
+            regroup(g, False)
         quantise(1)
         for g in range(NG):
             multiply(g)
             if g + 3 < NG:
-                transposes(g + 3)
+                transposes(g + 3, homes_of(g + 3))
             if g + 2 < NG:
                 quantise(g + 2)
             copy_out(g)
             if g + 3 < NG:
-                regroup(g + 3)
+                regroup(g + 3, False)

@@ -22,6 +22,7 @@ STORE_PLAN = (8, 8, 8, 8, 8, 8, 8, 4, 4)
 LOAD_SLOTS = (4, 4, 8, 16, 16, 16)
 SCALAR_OUT = (1, 3, 5)
 O_BUFS = 6
+AHEAD = 3
 
 FLOPS = 2 * TOKENS * N_OUT * K_IN
 BYTES = TOKENS * N_OUT * 2 + K_IN * N_OUT * 2 + TOKENS * K_IN * 4
@@ -39,6 +40,10 @@ def tile_binlinear_t_kernel(tc, x, w, grad_out, out):
         ctx.enter_context(tc.manual_schedule())
 
         w_sb = const.tile([P, 4 * N_OUT], BF16, name="w_sb")
+        nc.sync.dma_start(
+            out=w_sb[:].rearrange("p (t n) -> p t n", t=4),
+            in_=w.rearrange("(t p) n -> p t n", p=P),
+        )
         slot_home = []
         first = 0
         for i, count in enumerate(LOAD_SLOTS):
@@ -48,11 +53,6 @@ def tile_binlinear_t_kernel(tc, x, w, grad_out, out):
             for j in range(count):
                 slot_home.append((words, j * (N_OUT // 2)))
             first += count
-            if i == 0:
-                nc.sync.dma_start(
-                    out=w_sb[:].rearrange("p (t n) -> p t n", t=4),
-                    in_=w.rearrange("(t p) n -> p t n", p=P),
-                )
 
         ident = const.tile([P, P], F32, name="ident")
         make_identity(nc, ident[:])
@@ -144,13 +144,9 @@ def tile_binlinear_t_kernel(tc, x, w, grad_out, out):
         transposes(0, homes_of(0))
         regroup(0, False)
 
-        w_clip = const.tile([P, 4 * N_OUT], BF16, name="w_clip")
-        nc.vector.tensor_scalar(
-            out=w_clip[:], in0=w_sb[:], scalar1=-1.0, scalar2=1.0, op0=ALU.max, op1=ALU.min
-        )
         w_two = const.tile([P, 4 * N_OUT], BF16, name="w_two")
         nc.vector.tensor_scalar(
-            out=w_two[:], in0=w_clip[:], scalar1=0.0, scalar2=2.0, op0=ALU.is_ge, op1=ALU.mult
+            out=w_two[:], in0=w_sb[:], scalar1=0.0, scalar2=2.0, op0=ALU.is_ge, op1=ALU.mult
         )
         w_bin = const.tile([P, 4 * N_OUT], BF16, name="w_bin")
         nc.vector.tensor_scalar(
@@ -158,24 +154,25 @@ def tile_binlinear_t_kernel(tc, x, w, grad_out, out):
         )
         w_words = w_bin[:].bitcast(F32)
         transposes("w", [(w_words, t * (N_OUT // 2)) for t in range(4)])
-        quantise(0)
         regroup("w", True)
+        quantise(0)
         w_codes = const.tile([P, K_IN], U32, name="w_codes", align_bytes=64)
         w_scales = const.tile([P, K_IN], U8, name="w_scales", align_bytes=64)
         nc.vector.quantize_mx(
             out=w_codes[:].bitcast(E4M3X4), scales=w_scales[:], in_=grouped_of["w"][:]
         )
+        transposes(1, homes_of(1))
+        regroup(1, False)
 
-        for g in (1, 2):
-            transposes(g, homes_of(g))
-            regroup(g, False)
-        quantise(1)
+        issued = 2
         for g in range(NG):
             multiply(g)
-            if g + 3 < NG:
-                transposes(g + 3, homes_of(g + 3))
-            if g + 2 < NG:
-                quantise(g + 2)
+            fresh = list(range(issued, min(NG, g + AHEAD + 1)))
+            issued += len(fresh)
+            for f in fresh:
+                transposes(f, homes_of(f))
+            if g + 1 < NG:
+                quantise(g + 1)
             copy_out(g)
-            if g + 3 < NG:
-                regroup(g + 3, False)
+            for f in fresh:
+                regroup(f, False)

from contextlib import ExitStack

import concourse.mybir as mybir
from concourse.masks import make_identity

BF16 = mybir.dt.bfloat16
F32 = mybir.dt.float32
U32 = mybir.dt.uint32
U8 = mybir.dt.uint8
E5M2X4 = mybir.dt.float8_e5m2_x4
E4M3X4 = mybir.dt.float8_e4m3fn_x4
ALU = mybir.AluOpType

P = 128
TOKENS = 8192
N_OUT = 512
K_IN = 512
SLOTS = TOKENS // P
G = 4
NG = SLOTS // G
STORE_PLAN = (8, 8, 8, 8, 8, 8, 8, 4, 4)
LOAD_SLOTS = (4, 4, 8, 16, 16, 16)
SCALAR_OUT = (1, 3, 5)
O_BUFS = 6
AHEAD = 3

FLOPS = 2 * TOKENS * N_OUT * K_IN
BYTES = TOKENS * N_OUT * 2 + K_IN * N_OUT * 2 + TOKENS * K_IN * 4


def tile_binlinear_t_kernel(tc, x, w, grad_out, out):
    nc = tc.nc
    g_view = grad_out.rearrange("(p s) n -> p (s n)", s=SLOTS)
    o_view = out.rearrange("(p s) k -> p (s k)", s=SLOTS)
    with ExitStack() as ctx:
        const = ctx.enter_context(tc.tile_pool(name="const", bufs=1))
        stage = ctx.enter_context(tc.tile_pool(name="stage", bufs=4))
        outs = ctx.enter_context(tc.tile_pool(name="outs", bufs=O_BUFS))
        psum = ctx.enter_context(tc.psum_pool(name="psum", bufs=4))
        ctx.enter_context(tc.manual_schedule())

        w_sb = const.tile([P, 4 * N_OUT], BF16, name="w_sb")
        nc.sync.dma_start(
            out=w_sb[:].rearrange("p (t n) -> p t n", t=4),
            in_=w.rearrange("(t p) n -> p t n", p=P),
        )
        slot_home = []
        first = 0
        for i, count in enumerate(LOAD_SLOTS):
            g_sb = const.tile([P, count * N_OUT], BF16, name="g_sb%d" % i)
            nc.sync.dma_start(out=g_sb[:], in_=g_view[:, first * N_OUT : (first + count) * N_OUT])
            words = g_sb[:].bitcast(F32)
            for j in range(count):
                slot_home.append((words, j * (N_OUT // 2)))
            first += count

        ident = const.tile([P, P], F32, name="ident")
        make_identity(nc, ident[:])

        banks_of = {}
        grouped_of = {}
        mx_of = {}
        acc_of = {}
        o_of = {}

        def transposes(g, homes):
            banks = []
            for b in range(G // 2):
                xt = psum.tile([P, 512], F32, tag="xt")
                for a in range(2):
                    words, col = homes[2 * b + a]
                    for u in range(2):
                        nc.tensor.transpose(
                            out=xt[:, (2 * a + u) * P : (2 * a + u + 1) * P],
                            in_=words[:, col + u * P : col + (u + 1) * P],
                            identity=ident[:],
                        )
                banks.append(xt)
            banks_of[g] = banks

        def regroup(g, share):
            grouped = stage.tile([P, G * 512], BF16, tag="grouped", align_bytes=64)
            gw = grouped[:].bitcast(F32)
            for b, xt in enumerate(banks_of[g]):
                dst = gw[:, b * 512 : (b + 1) * 512].rearrange("p (a r u) -> p a r u", a=2, u=2)
                src = xt[:].rearrange("p (a u r) -> p a r u", a=2, u=2)
                if share and b == 0:
                    nc.vector.tensor_copy(out=dst, in_=src)
                else:
                    nc.scalar.copy(out=dst, in_=src)
            grouped_of[g] = grouped

        def quantise(g):
            codes = stage.tile([P, G * P], U32, tag="codes", align_bytes=64)
            scales = stage.tile([P, G * P], U8, tag="scales", align_bytes=64)
            nc.vector.quantize_mx(
                out=codes[:].bitcast(E5M2X4), scales=scales[:], in_=grouped_of[g][:]
            )
            mx_of[g] = (codes, scales)

        def multiply(g):
            codes, scales = mx_of[g]
            accs = []
            for a in range(G):
                acc = psum.tile([P, K_IN], F32, tag="acc")
                nc.tensor.matmul_mx(
                    out=acc[:],
                    lhsT=codes[:, a * P : (a + 1) * P].bitcast(E5M2X4),
                    lhsT_scale=scales[:, a * P : (a + 1) * P],
                    rhs=w_codes[:].bitcast(E4M3X4),
                    rhs_scale=w_scales[:],
                    start=True,
                    stop=True,
                )
                accs.append(acc)
            acc_of[g] = accs

        store_of = []
        for chunk, count in enumerate(STORE_PLAN):
            for j in range(count):
                store_of.append((chunk, j, count))

        def copy_out(g):
            for a, acc in enumerate(acc_of[g]):
                slot = g * G + a
                chunk, j, count = store_of[slot]
                if j == 0:
                    o_sb = outs.tile([P, count * K_IN], F32, tag="o_sb")
                    o_of[chunk] = o_sb
                dst = o_of[chunk][:, j * K_IN : (j + 1) * K_IN]
                if slot % 8 in SCALAR_OUT:
                    nc.scalar.copy(out=dst, in_=acc[:])
                else:
                    nc.vector.tensor_copy(out=dst, in_=acc[:])
                if j == count - 1:
                    nc.sync.dma_start(
                        out=o_view[:, (slot + 1 - count) * K_IN : (slot + 1) * K_IN],
                        in_=o_of[chunk][:],
                    )

        def homes_of(g):
            return slot_home[g * G : (g + 1) * G]

        transposes(0, homes_of(0))
        regroup(0, False)

        w_two = const.tile([P, 4 * N_OUT], BF16, name="w_two")
        nc.vector.tensor_scalar(
            out=w_two[:], in0=w_sb[:], scalar1=0.0, scalar2=2.0, op0=ALU.is_ge, op1=ALU.mult
        )
        w_bin = const.tile([P, 4 * N_OUT], BF16, name="w_bin")
        nc.vector.tensor_scalar(
            out=w_bin[:], in0=w_two[:], scalar1=-1.0, scalar2=None, op0=ALU.add
        )
        w_words = w_bin[:].bitcast(F32)
        transposes("w", [(w_words, t * (N_OUT // 2)) for t in range(4)])
        regroup("w", True)
        quantise(0)
        w_codes = const.tile([P, K_IN], U32, name="w_codes", align_bytes=64)
        w_scales = const.tile([P, K_IN], U8, name="w_scales", align_bytes=64)
        nc.vector.quantize_mx(
            out=w_codes[:].bitcast(E4M3X4), scales=w_scales[:], in_=grouped_of["w"][:]
        )
        transposes(1, homes_of(1))
        regroup(1, False)

        issued = 2
        for g in range(NG):
            multiply(g)
            fresh = list(range(issued, min(NG, g + AHEAD + 1)))
            issued += len(fresh)
            for f in fresh:
                transposes(f, homes_of(f))
            if g + 1 < NG:
                quantise(g + 1)
            copy_out(g)
            for f in fresh:
                regroup(f, False)
